import numpy as np
import ml_dtypes


def mxq(x, axis, fmt="e4m3"):
    dtype, down = {"e4m3": (ml_dtypes.float8_e4m3fn, 7), "e5m2": (ml_dtypes.float8_e5m2, 14)}[fmt]
    v = np.moveaxis(np.asarray(x, np.float32).astype(ml_dtypes.bfloat16).astype(np.float64), axis, -1)
    blocks = v.reshape(v.shape[:-1] + (-1, 32))
    amax = np.abs(blocks).max(-1, keepdims=True)
    byte = np.maximum(np.where(amax > 0, np.frexp(amax)[1] - 1 + 127, 0) - down, 1)
    scale = np.exp2(byte - 127.0)
    codes = (blocks / scale).astype(np.float32).astype(dtype).astype(np.float64)
    return np.moveaxis((codes * scale).reshape(v.shape), -1, axis)


WIDE = False


def mx_kscale(k):
    if not WIDE:
        return np.ones(k)
    levels = np.array([10, -10, 5, -5, 0])
    a = np.random.permutation(np.resize(levels, k // 512 * 4)).reshape(k // 512, 4)
    idx = np.arange(k)
    return np.exp2(a[idx // 512, idx % 128 // 32])


BF16 = ml_dtypes.bfloat16


def bf(x):
    return np.asarray(x, np.float32).astype(BF16)


def f64(x):
    return np.asarray(x).astype(np.float64)


E2M1 = np.array([0.0, 0.5, 1.0, 1.5, 2.0, 3.0, 4.0, 6.0, -0.0, -0.5, -1.0, -1.5, -2.0, -3.0, -4.0, -6.0])


def pack_weight(w, fmt):
    k, n = w.shape
    w = f64(bf(w)).reshape(k // 32, 32, n)
    amax = np.abs(w).max(1)
    if fmt == "e4m3":
        byte = np.frexp(amax)[1] - 1 + 127 - 7
    else:
        mant, ex = np.frexp(amax / 6.0)
        byte = np.where(mant > 0.5, ex, ex - 1) + 127
    byte = np.clip(np.where(amax > 0, byte, 1), 1, 254)
    scaled = (w * np.exp2(127.0 - byte)[:, None, :]).reshape(k, n).astype(np.float32)
    by_word = np.ascontiguousarray(scaled.reshape(k // 512, 128, 4, n).transpose(0, 1, 3, 2))
    if fmt == "e4m3":
        words = by_word.astype(ml_dtypes.float8_e4m3fn).view(np.uint8)
    else:
        c = by_word.astype(ml_dtypes.float4_e2m1fn).view(np.uint8) & 0xF
        words = c[..., 0::2] | (c[..., 1::2] << 4)
    return np.ascontiguousarray(words), np.ascontiguousarray(byte.astype(np.uint8).reshape(k // 512, 16, n))


def unpack_weight(words, scales, fmt):
    g, p, n, _ = words.shape
    if fmt == "e4m3":
        vals = np.ascontiguousarray(words).view(ml_dtypes.float8_e4m3fn).astype(np.float64)
    else:
        nib = np.empty((g, p, n, 4), np.uint8)
        nib[..., 0::2] = words & 0xF
        nib[..., 1::2] = words >> 4
        vals = E2M1[nib]
    vals = vals * np.repeat(np.exp2(scales.astype(np.float64) - 127.0), 8, axis=1)[..., None]
    return vals.transpose(0, 1, 3, 2).reshape(g * 512, n)


N, T, D, B0, C, P0, V1, P1, V2 = 2, 512, 1024, 2046, 2, 512, 2048, 512, 1024
SIG = 2.0
FMT = "e4m3"


def softmax(v):
    e = np.exp(v - v.max(-1, keepdims=True))
    return e / e.sum(-1, keepdims=True)


def setup_inputs():
    s, t = mx_kscale(D), mx_kscale(P1)
    x = bf(np.random.standard_normal((N, T, D)) * s)
    tail_proj_1_words, tail_proj_1_scales = pack_weight(np.random.standard_normal((D, P1)) / np.sqrt(D) / s[:, None] * t, FMT)
    tail_w_1_words, tail_w_1_scales = pack_weight(np.random.standard_normal((P1, V2)) * SIG / np.sqrt(P1) / t[:, None], FMT)
    cluster_prob = bf(1.0 / (1.0 + np.exp(0.7 - 1.5 * np.random.standard_normal((N, T, 1)))))
    return {"x": x,
            "tail_proj_1_words": tail_proj_1_words,
            "tail_proj_1_scales": tail_proj_1_scales,
            "tail_w_1_words": tail_w_1_words,
            "tail_w_1_scales": tail_w_1_scales,
            "cluster_prob": cluster_prob}


def reference(x, tail_proj_1_words, tail_proj_1_scales, tail_w_1_words, tail_w_1_scales, cluster_prob):
    h = mxq(f64(x), 2, "e4m3") @ unpack_weight(tail_proj_1_words, tail_proj_1_scales, FMT)
    tail_sm = softmax(mxq(h, 2, "e4m3") @ unpack_weight(tail_w_1_words, tail_w_1_scales, FMT))
    return tail_sm * f64(cluster_prob)

@@ -1,0 +1,195 @@
+from contextlib import ExitStack
+
+import concourse.mybir as mybir
+from concourse.masks import make_identity
+
+F32 = mybir.dt.float32
+BF16 = mybir.dt.bfloat16
+I32 = mybir.dt.int32
+U32 = mybir.dt.uint32
+U8 = mybir.dt.uint8
+FP8X4 = mybir.dt.float8_e4m3fn_x4
+ALU = mybir.AluOpType
+ACT = mybir.ActivationFunctionType
+AXIS = mybir.AxisListType
+
+P = 128
+PACK = 4
+K_PASS = P * PACK
+BANK = 512
+
+TOKENS = 1024
+D_MODEL = 1024
+D_TAIL = 512
+VOCAB = 1024
+TILES = TOKENS // P
+X_PASSES = D_MODEL // K_PASS
+HALVES = VOCAB // BANK
+
+FLOPS = 2 * TOKENS * D_MODEL * D_TAIL + 2 * TOKENS * D_TAIL * VOCAB
+
+
+def tile_adaptiveinputsoftmax_pb_kernel(
+    tc,
+    x,
+    tail_proj_1_words,
+    tail_proj_1_scales,
+    tail_w_1_words,
+    tail_w_1_scales,
+    cluster_prob,
+    out,
+):
+    nc = tc.nc
+
+    x_rows = x.flatten_outer_dims().rearrange("(p j) d -> p j d", j=TILES)
+    out_rows = out.flatten_outer_dims().rearrange("(p j) v -> p j v", j=TILES)
+    prob_rows = cluster_prob.flatten_outer_dims().rearrange("(p j) o -> p (j o)", j=TILES)
+
+    with ExitStack() as ctx:
+        keep = ctx.enter_context(tc.tile_pool(name="keep", bufs=1))
+        stage = ctx.enter_context(tc.tile_pool(name="stage", bufs=3))
+        small = ctx.enter_context(tc.tile_pool(name="small", bufs=4))
+        results = ctx.enter_context(tc.tile_pool(name="results", bufs=4))
+        psum_x = ctx.enter_context(tc.psum_pool(name="psum_x", bufs=2))
+        psum_h = ctx.enter_context(tc.psum_pool(name="psum_h", bufs=1))
+        psum_logits = ctx.enter_context(tc.psum_pool(name="psum_logits", bufs=2))
+
+        ident_f32 = keep.tile([P, P], F32)
+        make_identity(nc, ident_f32[:])
+        ident_bf16 = keep.tile([P, P], BF16)
+        make_identity(nc, ident_bf16[:])
+
+        planes = keep.tile([P, BANK], U8, align_bytes=64)
+        nc.vector.memset(planes[:].bitcast(I32), 0)
+
+        x_sb = keep.tile([P, TILES, D_MODEL], BF16)
+        w1_codes = keep.tile([P, X_PASSES, D_TAIL], U32, align_bytes=64)
+        w2_codes = keep.tile([P, VOCAB], U32, align_bytes=64)
+        prob_bf16 = keep.tile([P, TILES], BF16)
+        prob = keep.tile([P, TILES], F32)
+        x_codes = keep.tile([P, TILES, X_PASSES, P], U32, align_bytes=64)
+        x_scales = keep.tile([P, TILES, X_PASSES, P], U8, align_bytes=64)
+
+        w1_scale_rows = tail_proj_1_scales.bitcast(I32)
+        w2_scale_rows = tail_w_1_scales.bitcast(I32)
+
+        nc.sync.dma_start(out=x_sb[:, 0, :], in_=x_rows[:, 0, :])
+        nc.sync.dma_start(out=x_sb[:, 1, :], in_=x_rows[:, 1, :])
+        nc.sync.dma_start(
+            out=w1_codes[:].bitcast(I32),
+            in_=tail_proj_1_words.rearrange("g p n t -> p g (n t)").bitcast(I32),
+        )
+        for quadrant in range(4):
+            nc.sync.dma_start(
+                out=planes[32 * quadrant : 32 * quadrant + 8, :].bitcast(I32),
+                in_=w1_scale_rows[:, 4 * quadrant : 4 * quadrant + 4, :],
+            )
+        nc.sync.dma_start(out=x_sb[:, 2:4, :], in_=x_rows[:, 2:4, :])
+        nc.sync.dma_start(out=x_sb[:, 4:6, :], in_=x_rows[:, 4:6, :])
+        nc.sync.dma_start(
+            out=w2_codes[:].bitcast(I32),
+            in_=tail_w_1_words[0].rearrange("p n t -> p (n t)").bitcast(I32),
+        )
+        for quadrant in range(4):
+            nc.sync.dma_start(
+                out=planes[32 * quadrant + 8 : 32 * quadrant + 16, :].bitcast(I32),
+                in_=w2_scale_rows[0, 4 * quadrant : 4 * quadrant + 4, :].rearrange("r (h n) -> h r n", h=HALVES),
+            )
+        nc.sync.dma_start(out=x_sb[:, 6:8, :], in_=x_rows[:, 6:8, :])
+        nc.sync.dma_start(out=prob_bf16[:], in_=prob_rows)
+        nc.gpsimd.tensor_copy(out=prob[:], in_=prob_bf16[:])
+
+        for i in range(TILES):
+            x_words = x_sb[:, i, :].bitcast(F32)
+            x_t = psum_x.tile([P, X_PASSES, 2, P], F32)
+            for g in range(X_PASSES):
+                for u in range(2):
+                    nc.tensor.transpose(
+                        x_t[:, g, u, :],
+                        x_words[:, 256 * g + u : 256 * (g + 1) : 2],
+                        ident_f32[:],
+                    )
+            x_grouped = stage.tile([P, X_PASSES, P, PACK], BF16, align_bytes=64)
+            nc.vector.tensor_copy(
+                out=x_grouped[:].bitcast(F32),
+                in_=x_t[:].rearrange("p g u r -> p g r u"),
+            )
+            nc.vector.quantize_mx(
+                out=x_codes[:, i, :, :].rearrange("p g r -> p (g r)").bitcast(FP8X4),
+                scales=x_scales[:, i, :, :].rearrange("p g r -> p (g r)"),
+                in_=x_grouped[:].rearrange("p g r t -> p (g r t)"),
+            )
+
+            h_acc = psum_h.tile([P, D_TAIL], F32)
+            for g in range(X_PASSES):
+                nc.tensor.matmul_mx(
+                    out=h_acc[:],
+                    lhsT=x_codes[:, i, g, :].bitcast(FP8X4),
+                    lhsT_scale=x_scales[:, i, g, :],
+                    rhs=w1_codes[:, g, :].bitcast(FP8X4),
+                    rhs_scale=planes[4 * g : P, :],
+                    start=(g == 0),
+                    stop=(g == X_PASSES - 1),
+                )
+            h_rounded = stage.tile([P, PACK, P], BF16)
+            nc.scalar.copy(out=h_rounded[:], in_=h_acc[:].rearrange("r (p t) -> r t p", t=PACK))
+            h_t = psum_h.tile([P, PACK, P], BF16)
+            for t in range(PACK):
+                nc.tensor.transpose(h_t[:, t, :], h_rounded[:, t, :], ident_bf16[:])
+            h_grouped = stage.tile([P, P, PACK], BF16, align_bytes=64)
+            nc.scalar.copy(out=h_grouped[:], in_=h_t[:].rearrange("p t r -> p r t"))
+            h_codes = stage.tile([P, P], U32, align_bytes=64)
+            h_scales = stage.tile([P, P], U8, align_bytes=64)
+            nc.vector.quantize_mx(
+                out=h_codes[:].bitcast(FP8X4),
+                scales=h_scales[:],
+                in_=h_grouped[:].rearrange("p r t -> p (r t)"),
+            )
+
+            maxima = small.tile([P, HALVES], F32)
+            sums = small.tile([P, HALVES], F32)
+            neg_max = small.tile([P, 1], F32)
+            total = small.tile([P, 1], F32)
+            inverse = small.tile([P, 1], F32)
+            result = results.tile([P, VOCAB], F32)
+            logits = []
+            for half in range(HALVES):
+                bank = psum_logits.tile([P, BANK], F32, name="logits%d" % half)
+                logits.append(bank)
+                nc.tensor.matmul_mx(
+                    out=bank[:],
+                    lhsT=h_codes[:].bitcast(FP8X4),
+                    lhsT_scale=h_scales[:],
+                    rhs=w2_codes[:, BANK * half : BANK * (half + 1)].bitcast(FP8X4),
+                    rhs_scale=planes[8 + 4 * half : P, :],
+                    start=True,
+                    stop=True,
+                )
+                nc.vector.tensor_reduce(out=maxima[:, half : half + 1], in_=bank[:], axis=AXIS.X, op=ALU.max)
+            nc.vector.tensor_scalar(
+                out=neg_max[:],
+                in0=maxima[:, 0:1],
+                scalar1=maxima[:, 1:2],
+                scalar2=-1.0,
+                op0=ALU.max,
+                op1=ALU.mult,
+            )
+            for half in range(HALVES):
+                nc.scalar.activation(
+                    out=result[:, BANK * half : BANK * (half + 1)],
+                    in_=logits[half][:],
+                    func=ACT.Exp,
+                    bias=neg_max[:, 0:1],
+                    accum_out=sums[:, half : half + 1],
+                )
+            nc.vector.tensor_tensor(out=total[:], in0=sums[:, 0:1], in1=sums[:, 1:2], op=ALU.add)
+            nc.vector.reciprocal(inverse[:], total[:])
+            nc.vector.tensor_scalar(
+                out=result[:],
+                in0=result[:],
+                scalar1=inverse[:, 0:1],
+                scalar2=prob[:, i : i + 1],
+                op0=ALU.mult,
+                op1=ALU.mult,
+            )
+            nc.sync.dma_start(out=out_rows[:, i, :], in_=result[:])

@@ -26,6 +26,9 @@ TILES = TOKENS // P
 X_PASSES = D_MODEL // K_PASS
 HALVES = VOCAB // BANK
 
+X_PER_STEP = 2
+FIRST_STEP = -5
+
 FLOPS = 2 * TOKENS * D_MODEL * D_TAIL + 2 * TOKENS * D_TAIL * VOCAB
 
 
@@ -74,16 +77,16 @@ def tile_adaptiveinputsoftmax_pb_kernel(
         w2_scale_rows = tail_w_1_scales.bitcast(I32)
 
         nc.sync.dma_start(out=x_sb[:, 0, :], in_=x_rows[:, 0, :])
-        nc.sync.dma_start(out=x_sb[:, 1, :], in_=x_rows[:, 1, :])
-        nc.sync.dma_start(
-            out=w1_codes[:].bitcast(I32),
-            in_=tail_proj_1_words.rearrange("g p n t -> p g (n t)").bitcast(I32),
-        )
         for quadrant in range(4):
             nc.sync.dma_start(
                 out=planes[32 * quadrant : 32 * quadrant + 8, :].bitcast(I32),
                 in_=w1_scale_rows[:, 4 * quadrant : 4 * quadrant + 4, :],
             )
+        nc.sync.dma_start(
+            out=w1_codes[:].bitcast(I32),
+            in_=tail_proj_1_words.rearrange("g p n t -> p g (n t)").bitcast(I32),
+        )
+        nc.sync.dma_start(out=x_sb[:, 1, :], in_=x_rows[:, 1, :])
         nc.sync.dma_start(out=x_sb[:, 2:4, :], in_=x_rows[:, 2:4, :])
         nc.sync.dma_start(out=x_sb[:, 4:6, :], in_=x_rows[:, 4:6, :])
         nc.sync.dma_start(
@@ -99,31 +102,51 @@ def tile_adaptiveinputsoftmax_pb_kernel(
         nc.sync.dma_start(out=prob_bf16[:], in_=prob_rows)
         nc.gpsimd.tensor_copy(out=prob[:], in_=prob_bf16[:])
 
-        for i in range(TILES):
+        x_t = {}
+        x_grouped = {}
+        h_acc = {}
+        h_rounded = {}
+        h_t = {}
+        h_grouped = {}
+        h_codes = {}
+        h_scales = {}
+        logits = {}
+        neg_max = {}
+        sums = {}
+        result = {}
+
+        def transpose_x(i):
             x_words = x_sb[:, i, :].bitcast(F32)
-            x_t = psum_x.tile([P, X_PASSES, 2, P], F32)
+            x_t[i] = psum_x.tile([P, X_PASSES, 2, P], F32, name="x_t")
             for g in range(X_PASSES):
                 for u in range(2):
                     nc.tensor.transpose(
-                        x_t[:, g, u, :],
+                        x_t[i][:, g, u, :],
                         x_words[:, 256 * g + u : 256 * (g + 1) : 2],
                         ident_f32[:],
                     )
-            x_grouped = stage.tile([P, X_PASSES, P, PACK], BF16, align_bytes=64)
-            nc.vector.tensor_copy(
-                out=x_grouped[:].bitcast(F32),
-                in_=x_t[:].rearrange("p g u r -> p g r u"),
-            )
+
+        def regroup_x(i):
+            x_grouped[i] = stage.tile([P, X_PASSES, P, PACK], BF16, name="x_grouped", align_bytes=64)
+            words_out = x_grouped[i][:].bitcast(F32)
+            words_in = x_t[i][:].rearrange("p g u r -> p g r u")
+            if i % 2 == 0:
+                nc.vector.tensor_copy(out=words_out, in_=words_in)
+            else:
+                nc.scalar.copy(out=words_out, in_=words_in)
+
+        def quantise_x(i):
             nc.vector.quantize_mx(
                 out=x_codes[:, i, :, :].rearrange("p g r -> p (g r)").bitcast(FP8X4),
                 scales=x_scales[:, i, :, :].rearrange("p g r -> p (g r)"),
-                in_=x_grouped[:].rearrange("p g r t -> p (g r t)"),
+                in_=x_grouped[i][:].rearrange("p g r t -> p (g r t)"),
             )
 
-            h_acc = psum_h.tile([P, D_TAIL], F32)
+        def project(i):
+            h_acc[i] = psum_h.tile([P, D_TAIL], F32, name="h_acc")
             for g in range(X_PASSES):
                 nc.tensor.matmul_mx(
-                    out=h_acc[:],
+                    out=h_acc[i][:],
                     lhsT=x_codes[:, i, g, :].bitcast(FP8X4),
                     lhsT_scale=x_scales[:, i, g, :],
                     rhs=w1_codes[:, g, :].bitcast(FP8X4),
@@ -131,65 +154,112 @@ def tile_adaptiveinputsoftmax_pb_kernel(
                     start=(g == 0),
                     stop=(g == X_PASSES - 1),
                 )
-            h_rounded = stage.tile([P, PACK, P], BF16)
-            nc.scalar.copy(out=h_rounded[:], in_=h_acc[:].rearrange("r (p t) -> r t p", t=PACK))
-            h_t = psum_h.tile([P, PACK, P], BF16)
+
+        def round_h(i):
+            h_rounded[i] = stage.tile([P, PACK, P], BF16, name="h_rounded")
+            nc.scalar.copy(out=h_rounded[i][:], in_=h_acc[i][:].rearrange("r (p t) -> r t p", t=PACK))
+
+        def transpose_h(i):
+            h_t[i] = psum_h.tile([P, PACK, P], BF16, name="h_t")
             for t in range(PACK):
-                nc.tensor.transpose(h_t[:, t, :], h_rounded[:, t, :], ident_bf16[:])
-            h_grouped = stage.tile([P, P, PACK], BF16, align_bytes=64)
-            nc.scalar.copy(out=h_grouped[:], in_=h_t[:].rearrange("p t r -> p r t"))
-            h_codes = stage.tile([P, P], U32, align_bytes=64)
-            h_scales = stage.tile([P, P], U8, align_bytes=64)
+                nc.tensor.transpose(h_t[i][:, t, :], h_rounded[i][:, t, :], ident_bf16[:])
+
+        def regroup_h(i):
+            h_grouped[i] = stage.tile([P, P, PACK], BF16, name="h_grouped", align_bytes=64)
+            nc.scalar.copy(out=h_grouped[i][:], in_=h_t[i][:].rearrange("p t r -> p r t"))
+
+        def quantise_h(i):
+            h_codes[i] = stage.tile([P, P], U32, name="h_codes", align_bytes=64)
+            h_scales[i] = stage.tile([P, P], U8, name="h_scales", align_bytes=64)
             nc.vector.quantize_mx(
-                out=h_codes[:].bitcast(FP8X4),
-                scales=h_scales[:],
-                in_=h_grouped[:].rearrange("p r t -> p (r t)"),
+                out=h_codes[i][:].bitcast(FP8X4),
+                scales=h_scales[i][:],
+                in_=h_grouped[i][:].rearrange("p r t -> p (r t)"),
             )
 
-            maxima = small.tile([P, HALVES], F32)
-            sums = small.tile([P, HALVES], F32)
-            neg_max = small.tile([P, 1], F32)
-            total = small.tile([P, 1], F32)
-            inverse = small.tile([P, 1], F32)
-            result = results.tile([P, VOCAB], F32)
-            logits = []
+        def multiply_logits(i):
+            logits[i] = []
             for half in range(HALVES):
                 bank = psum_logits.tile([P, BANK], F32, name="logits%d" % half)
-                logits.append(bank)
+                logits[i].append(bank)
                 nc.tensor.matmul_mx(
                     out=bank[:],
-                    lhsT=h_codes[:].bitcast(FP8X4),
-                    lhsT_scale=h_scales[:],
+                    lhsT=h_codes[i][:].bitcast(FP8X4),
+                    lhsT_scale=h_scales[i][:],
                     rhs=w2_codes[:, BANK * half : BANK * (half + 1)].bitcast(FP8X4),
                     rhs_scale=planes[8 + 4 * half : P, :],
                     start=True,
                     stop=True,
                 )
-                nc.vector.tensor_reduce(out=maxima[:, half : half + 1], in_=bank[:], axis=AXIS.X, op=ALU.max)
+
+        def row_max(i):
+            maxima = small.tile([P, HALVES], F32, name="maxima")
+            for half in range(HALVES):
+                nc.vector.tensor_reduce(out=maxima[:, half : half + 1], in_=logits[i][half][:], axis=AXIS.X, op=ALU.max)
+            neg_max[i] = small.tile([P, 1], F32, name="neg_max")
             nc.vector.tensor_scalar(
-                out=neg_max[:],
+                out=neg_max[i][:],
                 in0=maxima[:, 0:1],
                 scalar1=maxima[:, 1:2],
                 scalar2=-1.0,
                 op0=ALU.max,
                 op1=ALU.mult,
             )
+
+        def exponentials(i):
+            sums[i] = small.tile([P, HALVES], F32, name="sums")
+            result[i] = results.tile([P, VOCAB], F32, name="result")
             for half in range(HALVES):
                 nc.scalar.activation(
-                    out=result[:, BANK * half : BANK * (half + 1)],
-                    in_=logits[half][:],
+                    out=result[i][:, BANK * half : BANK * (half + 1)],
+                    in_=logits[i][half][:],
                     func=ACT.Exp,
-                    bias=neg_max[:, 0:1],
-                    accum_out=sums[:, half : half + 1],
+                    bias=neg_max[i][:, 0:1],
+                    accum_out=sums[i][:, half : half + 1],
                 )
-            nc.vector.tensor_tensor(out=total[:], in0=sums[:, 0:1], in1=sums[:, 1:2], op=ALU.add)
+
+        def normalise_and_store(i):
+            total = small.tile([P, 1], F32, name="total")
+            inverse = small.tile([P, 1], F32, name="inverse")
+            nc.vector.tensor_tensor(out=total[:], in0=sums[i][:, 0:1], in1=sums[i][:, 1:2], op=ALU.add)
             nc.vector.reciprocal(inverse[:], total[:])
             nc.vector.tensor_scalar(
-                out=result[:],
-                in0=result[:],
+                out=result[i][:],
+                in0=result[i][:],
                 scalar1=inverse[:, 0:1],
                 scalar2=prob[:, i : i + 1],
                 op0=ALU.mult,
                 op1=ALU.mult,
             )
-            nc.sync.dma_start(out=out_rows[:, i, :], in_=result[:])
+            nc.sync.dma_start(out=out_rows[:, i, :], in_=result[i][:])
+
+        def in_range(i):
+            return 0 <= i < TILES
+
+        with tc.manual_schedule():
+            for step in range(FIRST_STEP, TILES):
+                first_x = X_PER_STEP * (step - FIRST_STEP)
+                x_tiles = [i for i in range(first_x, first_x + X_PER_STEP) if in_range(i)]
+                if in_range(step):
+                    exponentials(step)
+                if in_range(step + 3):
+                    transpose_h(step + 3)
+                    regroup_h(step + 3)
+                if in_range(step + 4):
+                    project(step + 4)
+                if in_range(step + 2):
+                    multiply_logits(step + 2)
+                for i in x_tiles:
+                    transpose_x(i)
+                if in_range(step + 3):
+                    quantise_h(step + 3)
+                if in_range(step + 4):
+                    round_h(step + 4)
+                for i in x_tiles:
+                    regroup_x(i)
+                if in_range(step + 2):
+                    row_max(step + 2)
+                for i in x_tiles:
+                    quantise_x(i)
+                if in_range(step):
+                    normalise_and_store(step)

@@ -26,9 +26,6 @@ TILES = TOKENS // P
 X_PASSES = D_MODEL // K_PASS
 HALVES = VOCAB // BANK
 
-X_PER_STEP = 2
-FIRST_STEP = -5
-
 FLOPS = 2 * TOKENS * D_MODEL * D_TAIL + 2 * TOKENS * D_TAIL * VOCAB
 
 
@@ -50,11 +47,10 @@ def tile_adaptiveinputsoftmax_pb_kernel(
 
     with ExitStack() as ctx:
         keep = ctx.enter_context(tc.tile_pool(name="keep", bufs=1))
-        stage = ctx.enter_context(tc.tile_pool(name="stage", bufs=3))
+        stage = ctx.enter_context(tc.tile_pool(name="stage", bufs=4))
         small = ctx.enter_context(tc.tile_pool(name="small", bufs=4))
         results = ctx.enter_context(tc.tile_pool(name="results", bufs=4))
-        psum_x = ctx.enter_context(tc.psum_pool(name="psum_x", bufs=2))
-        psum_h = ctx.enter_context(tc.psum_pool(name="psum_h", bufs=1))
+        psum_h = ctx.enter_context(tc.psum_pool(name="psum_h", bufs=2))
         psum_logits = ctx.enter_context(tc.psum_pool(name="psum_logits", bufs=2))
 
         ident_f32 = keep.tile([P, P], F32)
@@ -77,6 +73,7 @@ def tile_adaptiveinputsoftmax_pb_kernel(
         w2_scale_rows = tail_w_1_scales.bitcast(I32)
 
         nc.sync.dma_start(out=x_sb[:, 0, :], in_=x_rows[:, 0, :])
+        nc.sync.dma_start(out=x_sb[:, 1, :], in_=x_rows[:, 1, :])
         for quadrant in range(4):
             nc.sync.dma_start(
                 out=planes[32 * quadrant : 32 * quadrant + 8, :].bitcast(I32),
@@ -86,67 +83,47 @@ def tile_adaptiveinputsoftmax_pb_kernel(
             out=w1_codes[:].bitcast(I32),
             in_=tail_proj_1_words.rearrange("g p n t -> p g (n t)").bitcast(I32),
         )
-        nc.sync.dma_start(out=x_sb[:, 1, :], in_=x_rows[:, 1, :])
         nc.sync.dma_start(out=x_sb[:, 2:4, :], in_=x_rows[:, 2:4, :])
         nc.sync.dma_start(out=x_sb[:, 4:6, :], in_=x_rows[:, 4:6, :])
-        nc.sync.dma_start(
-            out=w2_codes[:].bitcast(I32),
-            in_=tail_w_1_words[0].rearrange("p n t -> p (n t)").bitcast(I32),
-        )
+        nc.sync.dma_start(out=x_sb[:, 6:8, :], in_=x_rows[:, 6:8, :])
         for quadrant in range(4):
             nc.sync.dma_start(
                 out=planes[32 * quadrant + 8 : 32 * quadrant + 16, :].bitcast(I32),
                 in_=w2_scale_rows[0, 4 * quadrant : 4 * quadrant + 4, :].rearrange("r (h n) -> h r n", h=HALVES),
             )
-        nc.sync.dma_start(out=x_sb[:, 6:8, :], in_=x_rows[:, 6:8, :])
+        nc.sync.dma_start(
+            out=w2_codes[:].bitcast(I32),
+            in_=tail_w_1_words[0].rearrange("p n t -> p (n t)").bitcast(I32),
+        )
         nc.sync.dma_start(out=prob_bf16[:], in_=prob_rows)
         nc.gpsimd.tensor_copy(out=prob[:], in_=prob_bf16[:])
 
-        x_t = {}
-        x_grouped = {}
-        h_acc = {}
-        h_rounded = {}
-        h_t = {}
-        h_grouped = {}
-        h_codes = {}
-        h_scales = {}
-        logits = {}
-        neg_max = {}
-        sums = {}
-        result = {}
-
-        def transpose_x(i):
+        for i in range(TILES):
             x_words = x_sb[:, i, :].bitcast(F32)
-            x_t[i] = psum_x.tile([P, X_PASSES, 2, P], F32, name="x_t")
+            x_t = psum_logits.tile([P, X_PASSES, 2, P], F32, tag="logits%d" % (i % HALVES))
             for g in range(X_PASSES):
                 for u in range(2):
                     nc.tensor.transpose(
-                        x_t[i][:, g, u, :],
+                        x_t[:, g, u, :],
                         x_words[:, 256 * g + u : 256 * (g + 1) : 2],
                         ident_f32[:],
                     )
-
-        def regroup_x(i):
-            x_grouped[i] = stage.tile([P, X_PASSES, P, PACK], BF16, name="x_grouped", align_bytes=64)
-            words_out = x_grouped[i][:].bitcast(F32)
-            words_in = x_t[i][:].rearrange("p g u r -> p g r u")
-            if i % 2 == 0:
-                nc.vector.tensor_copy(out=words_out, in_=words_in)
-            else:
-                nc.scalar.copy(out=words_out, in_=words_in)
-
-        def quantise_x(i):
+            x_grouped = stage.tile([P, X_PASSES, P, PACK], BF16, align_bytes=64)
+            nc.vector.tensor_copy(
+                out=x_grouped[:].bitcast(F32),
+                in_=x_t[:].rearrange("p g u r -> p g r u"),
+            )
             nc.vector.quantize_mx(
                 out=x_codes[:, i, :, :].rearrange("p g r -> p (g r)").bitcast(FP8X4),
                 scales=x_scales[:, i, :, :].rearrange("p g r -> p (g r)"),
-                in_=x_grouped[i][:].rearrange("p g r t -> p (g r t)"),
+                in_=x_grouped[:].rearrange("p g r t -> p (g r t)"),
             )
 
-        def project(i):
-            h_acc[i] = psum_h.tile([P, D_TAIL], F32, name="h_acc")
+        for i in range(TILES):
+            h_acc = psum_h.tile([P, D_TAIL], F32)
             for g in range(X_PASSES):
                 nc.tensor.matmul_mx(
-                    out=h_acc[i][:],
+                    out=h_acc[:],
                     lhsT=x_codes[:, i, g, :].bitcast(FP8X4),
                     lhsT_scale=x_scales[:, i, g, :],
                     rhs=w1_codes[:, g, :].bitcast(FP8X4),
@@ -154,112 +131,65 @@ def tile_adaptiveinputsoftmax_pb_kernel(
                     start=(g == 0),
                     stop=(g == X_PASSES - 1),
                 )
-
-        def round_h(i):
-            h_rounded[i] = stage.tile([P, PACK, P], BF16, name="h_rounded")
-            nc.scalar.copy(out=h_rounded[i][:], in_=h_acc[i][:].rearrange("r (p t) -> r t p", t=PACK))
-
-        def transpose_h(i):
-            h_t[i] = psum_h.tile([P, PACK, P], BF16, name="h_t")
+            h_rounded = stage.tile([P, PACK, P], BF16)
+            nc.scalar.copy(out=h_rounded[:], in_=h_acc[:].rearrange("r (p t) -> r t p", t=PACK))
+            h_t = psum_h.tile([P, PACK, P], BF16)
             for t in range(PACK):
-                nc.tensor.transpose(h_t[i][:, t, :], h_rounded[i][:, t, :], ident_bf16[:])
-
-        def regroup_h(i):
-            h_grouped[i] = stage.tile([P, P, PACK], BF16, name="h_grouped", align_bytes=64)
-            nc.scalar.copy(out=h_grouped[i][:], in_=h_t[i][:].rearrange("p t r -> p r t"))
-
-        def quantise_h(i):
-            h_codes[i] = stage.tile([P, P], U32, name="h_codes", align_bytes=64)
-            h_scales[i] = stage.tile([P, P], U8, name="h_scales", align_bytes=64)
+                nc.tensor.transpose(h_t[:, t, :], h_rounded[:, t, :], ident_bf16[:])
+            h_grouped = stage.tile([P, P, PACK], BF16, align_bytes=64)
+            nc.scalar.copy(out=h_grouped[:], in_=h_t[:].rearrange("p t r -> p r t"))
+            h_codes = stage.tile([P, P], U32, align_bytes=64)
+            h_scales = stage.tile([P, P], U8, align_bytes=64)
             nc.vector.quantize_mx(
-                out=h_codes[i][:].bitcast(FP8X4),
-                scales=h_scales[i][:],
-                in_=h_grouped[i][:].rearrange("p r t -> p (r t)"),
+                out=h_codes[:].bitcast(FP8X4),
+                scales=h_scales[:],
+                in_=h_grouped[:].rearrange("p r t -> p (r t)"),
             )
 
-        def multiply_logits(i):
-            logits[i] = []
+            maxima = small.tile([P, HALVES], F32)
+            sums = small.tile([P, HALVES], F32)
+            neg_max = small.tile([P, 1], F32)
+            total = small.tile([P, 1], F32)
+            inverse = small.tile([P, 1], F32)
+            result = results.tile([P, VOCAB], F32)
+            logits = []
             for half in range(HALVES):
-                bank = psum_logits.tile([P, BANK], F32, name="logits%d" % half)
-                logits[i].append(bank)
+                bank = psum_logits.tile([P, BANK], F32, tag="logits%d" % half)
+                logits.append(bank)
                 nc.tensor.matmul_mx(
                     out=bank[:],
-                    lhsT=h_codes[i][:].bitcast(FP8X4),
-                    lhsT_scale=h_scales[i][:],
+                    lhsT=h_codes[:].bitcast(FP8X4),
+                    lhsT_scale=h_scales[:],
                     rhs=w2_codes[:, BANK * half : BANK * (half + 1)].bitcast(FP8X4),
                     rhs_scale=planes[8 + 4 * half : P, :],
                     start=True,
                     stop=True,
                 )
-
-        def row_max(i):
-            maxima = small.tile([P, HALVES], F32, name="maxima")
-            for half in range(HALVES):
-                nc.vector.tensor_reduce(out=maxima[:, half : half + 1], in_=logits[i][half][:], axis=AXIS.X, op=ALU.max)
-            neg_max[i] = small.tile([P, 1], F32, name="neg_max")
+                nc.vector.tensor_reduce(out=maxima[:, half : half + 1], in_=bank[:], axis=AXIS.X, op=ALU.max)
             nc.vector.tensor_scalar(
-                out=neg_max[i][:],
+                out=neg_max[:],
                 in0=maxima[:, 0:1],
                 scalar1=maxima[:, 1:2],
                 scalar2=-1.0,
                 op0=ALU.max,
                 op1=ALU.mult,
             )
-
-        def exponentials(i):
-            sums[i] = small.tile([P, HALVES], F32, name="sums")
-            result[i] = results.tile([P, VOCAB], F32, name="result")
             for half in range(HALVES):
                 nc.scalar.activation(
-                    out=result[i][:, BANK * half : BANK * (half + 1)],
-                    in_=logits[i][half][:],
+                    out=result[:, BANK * half : BANK * (half + 1)],
+                    in_=logits[half][:],
                     func=ACT.Exp,
-                    bias=neg_max[i][:, 0:1],
-                    accum_out=sums[i][:, half : half + 1],
+                    bias=neg_max[:, 0:1],
+                    accum_out=sums[:, half : half + 1],
                 )
-
-        def normalise_and_store(i):
-            total = small.tile([P, 1], F32, name="total")
-            inverse = small.tile([P, 1], F32, name="inverse")
-            nc.vector.tensor_tensor(out=total[:], in0=sums[i][:, 0:1], in1=sums[i][:, 1:2], op=ALU.add)
+            nc.vector.tensor_tensor(out=total[:], in0=sums[:, 0:1], in1=sums[:, 1:2], op=ALU.add)
             nc.vector.reciprocal(inverse[:], total[:])
             nc.vector.tensor_scalar(
-                out=result[i][:],
-                in0=result[i][:],
+                out=result[:],
+                in0=result[:],
                 scalar1=inverse[:, 0:1],
                 scalar2=prob[:, i : i + 1],
                 op0=ALU.mult,
                 op1=ALU.mult,
             )
-            nc.sync.dma_start(out=out_rows[:, i, :], in_=result[i][:])
-
-        def in_range(i):
-            return 0 <= i < TILES
-
-        with tc.manual_schedule():
-            for step in range(FIRST_STEP, TILES):
-                first_x = X_PER_STEP * (step - FIRST_STEP)
-                x_tiles = [i for i in range(first_x, first_x + X_PER_STEP) if in_range(i)]
-                if in_range(step):
-                    exponentials(step)
-                if in_range(step + 3):
-                    transpose_h(step + 3)
-                    regroup_h(step + 3)
-                if in_range(step + 4):
-                    project(step + 4)
-                if in_range(step + 2):
-                    multiply_logits(step + 2)
-                for i in x_tiles:
-                    transpose_x(i)
-                if in_range(step + 3):
-                    quantise_h(step + 3)
-                if in_range(step + 4):
-                    round_h(step + 4)
-                for i in x_tiles:
-                    regroup_x(i)
-                if in_range(step + 2):
-                    row_max(step + 2)
-                for i in x_tiles:
-                    quantise_x(i)
-                if in_range(step):
-                    normalise_and_store(step)
+            nc.sync.dma_start(out=out_rows[:, i, :], in_=result[:])

@@ -50,19 +50,27 @@ def tile_adaptiveinputsoftmax_pb_kernel(
         stage = ctx.enter_context(tc.tile_pool(name="stage", bufs=4))
         small = ctx.enter_context(tc.tile_pool(name="small", bufs=4))
         results = ctx.enter_context(tc.tile_pool(name="results", bufs=4))
+        psum_x = ctx.enter_context(tc.psum_pool(name="psum_x", bufs=2))
         psum_h = ctx.enter_context(tc.psum_pool(name="psum_h", bufs=2))
         psum_logits = ctx.enter_context(tc.psum_pool(name="psum_logits", bufs=2))
 
         ident_f32 = keep.tile([P, P], F32)
         make_identity(nc, ident_f32[:])
-        ident_bf16 = keep.tile([P, P], BF16)
-        make_identity(nc, ident_bf16[:])
 
-        planes = keep.tile([P, BANK], U8, align_bytes=64)
-        nc.vector.memset(planes[:].bitcast(I32), 0)
+        warm_in = keep.tile([P, 1], F32)
+        warm_out = keep.tile([P, 1], F32)
+        nc.vector.memset(warm_in[:], 0.0)
+        nc.scalar.activation(out=warm_out[:], in_=warm_in[:], func=ACT.Exp)
+
+        w1_planes_raw = keep.tile([P, D_TAIL], U8, align_bytes=64)
+        w1_planes = keep.tile([P, D_TAIL], U8, align_bytes=64)
+        w2_planes = keep.tile([P, BANK], U8, align_bytes=64)
+        nc.vector.memset(w1_planes_raw[:].bitcast(I32), 0)
+        nc.vector.memset(w2_planes[:].bitcast(I32), 0)
 
         x_sb = keep.tile([P, TILES, D_MODEL], BF16)
-        w1_codes = keep.tile([P, X_PASSES, D_TAIL], U32, align_bytes=64)
+        w1_raw = keep.tile([P, X_PASSES, D_TAIL], U32, align_bytes=64)
+        w1_codes = keep.tile([P, X_PASSES, PACK, P], U32, align_bytes=64)
         w2_codes = keep.tile([P, VOCAB], U32, align_bytes=64)
         prob_bf16 = keep.tile([P, TILES], BF16)
         prob = keep.tile([P, TILES], F32)
@@ -73,34 +81,44 @@ def tile_adaptiveinputsoftmax_pb_kernel(
         w2_scale_rows = tail_w_1_scales.bitcast(I32)
 
         nc.sync.dma_start(out=x_sb[:, 0, :], in_=x_rows[:, 0, :])
-        nc.sync.dma_start(out=x_sb[:, 1, :], in_=x_rows[:, 1, :])
         for quadrant in range(4):
             nc.sync.dma_start(
-                out=planes[32 * quadrant : 32 * quadrant + 8, :].bitcast(I32),
+                out=w1_planes_raw[32 * quadrant : 32 * quadrant + 8, :].bitcast(I32),
                 in_=w1_scale_rows[:, 4 * quadrant : 4 * quadrant + 4, :],
             )
         nc.sync.dma_start(
-            out=w1_codes[:].bitcast(I32),
+            out=w1_raw[:].bitcast(I32),
             in_=tail_proj_1_words.rearrange("g p n t -> p g (n t)").bitcast(I32),
         )
-        nc.sync.dma_start(out=x_sb[:, 2:4, :], in_=x_rows[:, 2:4, :])
-        nc.sync.dma_start(out=x_sb[:, 4:6, :], in_=x_rows[:, 4:6, :])
-        nc.sync.dma_start(out=x_sb[:, 6:8, :], in_=x_rows[:, 6:8, :])
+        nc.sync.dma_start(out=x_sb[:, 1, :], in_=x_rows[:, 1, :])
         for quadrant in range(4):
             nc.sync.dma_start(
-                out=planes[32 * quadrant + 8 : 32 * quadrant + 16, :].bitcast(I32),
+                out=w2_planes[32 * quadrant : 32 * quadrant + 8, :].bitcast(I32),
                 in_=w2_scale_rows[0, 4 * quadrant : 4 * quadrant + 4, :].rearrange("r (h n) -> h r n", h=HALVES),
             )
         nc.sync.dma_start(
             out=w2_codes[:].bitcast(I32),
             in_=tail_w_1_words[0].rearrange("p n t -> p (n t)").bitcast(I32),
         )
+        nc.sync.dma_start(out=x_sb[:, 2:4, :], in_=x_rows[:, 2:4, :])
+        nc.sync.dma_start(out=x_sb[:, 4:6, :], in_=x_rows[:, 4:6, :])
+        nc.sync.dma_start(out=x_sb[:, 6:8, :], in_=x_rows[:, 6:8, :])
         nc.sync.dma_start(out=prob_bf16[:], in_=prob_rows)
         nc.gpsimd.tensor_copy(out=prob[:], in_=prob_bf16[:])
 
+        nc.vector.tensor_copy(
+            out=w1_planes[:].rearrange("p (t m) -> p m t", t=PACK),
+            in_=w1_planes_raw[:].rearrange("p (m t) -> p m t", t=PACK),
+        )
+        for g in range(X_PASSES):
+            nc.vector.tensor_copy(
+                out=w1_codes[:, g, :, :].bitcast(I32),
+                in_=w1_raw[:, g, :].bitcast(I32).rearrange("p (m t) -> p t m", t=PACK),
+            )
+
         for i in range(TILES):
             x_words = x_sb[:, i, :].bitcast(F32)
-            x_t = psum_logits.tile([P, X_PASSES, 2, P], F32, tag="logits%d" % (i % HALVES))
+            x_t = psum_x.tile([P, X_PASSES, 2, P], F32)
             for g in range(X_PASSES):
                 for u in range(2):
                     nc.tensor.transpose(
@@ -109,7 +127,7 @@ def tile_adaptiveinputsoftmax_pb_kernel(
                         ident_f32[:],
                     )
             x_grouped = stage.tile([P, X_PASSES, P, PACK], BF16, align_bytes=64)
-            nc.vector.tensor_copy(
+            nc.scalar.copy(
                 out=x_grouped[:].bitcast(F32),
                 in_=x_t[:].rearrange("p g u r -> p g r u"),
             )
@@ -120,22 +138,18 @@ def tile_adaptiveinputsoftmax_pb_kernel(
             )
 
         for i in range(TILES):
-            h_acc = psum_h.tile([P, D_TAIL], F32)
-            for g in range(X_PASSES):
-                nc.tensor.matmul_mx(
-                    out=h_acc[:],
-                    lhsT=x_codes[:, i, g, :].bitcast(FP8X4),
-                    lhsT_scale=x_scales[:, i, g, :],
-                    rhs=w1_codes[:, g, :].bitcast(FP8X4),
-                    rhs_scale=planes[4 * g : P, :],
-                    start=(g == 0),
-                    stop=(g == X_PASSES - 1),
-                )
-            h_rounded = stage.tile([P, PACK, P], BF16)
-            nc.scalar.copy(out=h_rounded[:], in_=h_acc[:].rearrange("r (p t) -> r t p", t=PACK))
-            h_t = psum_h.tile([P, PACK, P], BF16)
+            h_t = psum_h.tile([P, PACK, P], F32)
             for t in range(PACK):
-                nc.tensor.transpose(h_t[:, t, :], h_rounded[:, t, :], ident_bf16[:])
+                for g in range(X_PASSES):
+                    nc.tensor.matmul_mx(
+                        out=h_t[:, t, :],
+                        lhsT=w1_codes[:, g, t, :].bitcast(FP8X4),
+                        lhsT_scale=w1_planes[4 * g : P, P * t : P * (t + 1)],
+                        rhs=x_codes[:, i, g, :].bitcast(FP8X4),
+                        rhs_scale=x_scales[:, i, g, :],
+                        start=(g == 0),
+                        stop=(g == X_PASSES - 1),
+                    )
             h_grouped = stage.tile([P, P, PACK], BF16, align_bytes=64)
             nc.scalar.copy(out=h_grouped[:], in_=h_t[:].rearrange("p t r -> p r t"))
             h_codes = stage.tile([P, P], U32, align_bytes=64)
@@ -161,7 +175,7 @@ def tile_adaptiveinputsoftmax_pb_kernel(
                     lhsT=h_codes[:].bitcast(FP8X4),
                     lhsT_scale=h_scales[:],
                     rhs=w2_codes[:, BANK * half : BANK * (half + 1)].bitcast(FP8X4),
-                    rhs_scale=planes[8 + 4 * half : P, :],
+                    rhs_scale=w2_planes[4 * half : P, :],
                     start=True,
                     stop=True,
                 )

@@ -49,10 +49,11 @@ def tile_adaptiveinputsoftmax_pb_kernel(
         keep = ctx.enter_context(tc.tile_pool(name="keep", bufs=1))
         stage = ctx.enter_context(tc.tile_pool(name="stage", bufs=4))
         small = ctx.enter_context(tc.tile_pool(name="small", bufs=4))
-        results = ctx.enter_context(tc.tile_pool(name="results", bufs=4))
+        results = ctx.enter_context(tc.tile_pool(name="results", bufs=8))
         psum_x = ctx.enter_context(tc.psum_pool(name="psum_x", bufs=2))
         psum_h = ctx.enter_context(tc.psum_pool(name="psum_h", bufs=2))
         psum_logits = ctx.enter_context(tc.psum_pool(name="psum_logits", bufs=2))
+        ctx.enter_context(tc.manual_schedule())
 
         ident_f32 = keep.tile([P, P], F32)
         make_identity(nc, ident_f32[:])
@@ -86,11 +87,13 @@ def tile_adaptiveinputsoftmax_pb_kernel(
                 out=w1_planes_raw[32 * quadrant : 32 * quadrant + 8, :].bitcast(I32),
                 in_=w1_scale_rows[:, 4 * quadrant : 4 * quadrant + 4, :],
             )
-        nc.sync.dma_start(
-            out=w1_raw[:].bitcast(I32),
-            in_=tail_proj_1_words.rearrange("g p n t -> p g (n t)").bitcast(I32),
-        )
-        nc.sync.dma_start(out=x_sb[:, 1, :], in_=x_rows[:, 1, :])
+        for g in range(X_PASSES):
+            nc.sync.dma_start(
+                out=w1_raw[:, g, :].bitcast(I32),
+                in_=tail_proj_1_words[g].rearrange("p n t -> p (n t)").bitcast(I32),
+            )
+        for i in range(1, 4):
+            nc.sync.dma_start(out=x_sb[:, i, :], in_=x_rows[:, i, :])
         for quadrant in range(4):
             nc.sync.dma_start(
                 out=w2_planes[32 * quadrant : 32 * quadrant + 8, :].bitcast(I32),
@@ -100,10 +103,9 @@ def tile_adaptiveinputsoftmax_pb_kernel(
             out=w2_codes[:].bitcast(I32),
             in_=tail_w_1_words[0].rearrange("p n t -> p (n t)").bitcast(I32),
         )
-        nc.sync.dma_start(out=x_sb[:, 2:4, :], in_=x_rows[:, 2:4, :])
-        nc.sync.dma_start(out=x_sb[:, 4:6, :], in_=x_rows[:, 4:6, :])
-        nc.sync.dma_start(out=x_sb[:, 6:8, :], in_=x_rows[:, 6:8, :])
         nc.sync.dma_start(out=prob_bf16[:], in_=prob_rows)
+        for i in range(4, TILES):
+            nc.sync.dma_start(out=x_sb[:, i, :], in_=x_rows[:, i, :])
         nc.gpsimd.tensor_copy(out=prob[:], in_=prob_bf16[:])
 
         nc.vector.tensor_copy(
@@ -116,7 +118,9 @@ def tile_adaptiveinputsoftmax_pb_kernel(
                 in_=w1_raw[:, g, :].bitcast(I32).rearrange("p (m t) -> p t m", t=PACK),
             )
 
-        for i in range(TILES):
+        live = {}
+
+        def transpose_x(i):
             x_words = x_sb[:, i, :].bitcast(F32)
             x_t = psum_x.tile([P, X_PASSES, 2, P], F32)
             for g in range(X_PASSES):
@@ -126,18 +130,24 @@ def tile_adaptiveinputsoftmax_pb_kernel(
                         x_words[:, 256 * g + u : 256 * (g + 1) : 2],
                         ident_f32[:],
                     )
+            live["x_t", i] = x_t
+
+        def copy_x(i):
             x_grouped = stage.tile([P, X_PASSES, P, PACK], BF16, align_bytes=64)
             nc.scalar.copy(
                 out=x_grouped[:].bitcast(F32),
-                in_=x_t[:].rearrange("p g u r -> p g r u"),
+                in_=live["x_t", i][:].rearrange("p g u r -> p g r u"),
             )
+            live["x_grouped", i] = x_grouped
+
+        def quantize_x(i):
             nc.vector.quantize_mx(
                 out=x_codes[:, i, :, :].rearrange("p g r -> p (g r)").bitcast(FP8X4),
                 scales=x_scales[:, i, :, :].rearrange("p g r -> p (g r)"),
-                in_=x_grouped[:].rearrange("p g r t -> p (g r t)"),
+                in_=live["x_grouped", i][:].rearrange("p g r t -> p (g r t)"),
             )
 
-        for i in range(TILES):
+        def project(i):
             h_t = psum_h.tile([P, PACK, P], F32)
             for t in range(PACK):
                 for g in range(X_PASSES):
@@ -150,36 +160,47 @@ def tile_adaptiveinputsoftmax_pb_kernel(
                         start=(g == 0),
                         stop=(g == X_PASSES - 1),
                     )
+            live["h_t", i] = h_t
+
+        def copy_h(i):
             h_grouped = stage.tile([P, P, PACK], BF16, align_bytes=64)
-            nc.scalar.copy(out=h_grouped[:], in_=h_t[:].rearrange("p t r -> p r t"))
+            nc.scalar.copy(out=h_grouped[:], in_=live["h_t", i][:].rearrange("p t r -> p r t"))
+            live["h_grouped", i] = h_grouped
+
+        def quantize_h(i):
             h_codes = stage.tile([P, P], U32, align_bytes=64)
             h_scales = stage.tile([P, P], U8, align_bytes=64)
             nc.vector.quantize_mx(
                 out=h_codes[:].bitcast(FP8X4),
                 scales=h_scales[:],
-                in_=h_grouped[:].rearrange("p r t -> p (r t)"),
+                in_=live["h_grouped", i][:].rearrange("p r t -> p (r t)"),
             )
+            live["h_codes", i] = h_codes
+            live["h_scales", i] = h_scales
 
-            maxima = small.tile([P, HALVES], F32)
-            sums = small.tile([P, HALVES], F32)
-            neg_max = small.tile([P, 1], F32)
-            total = small.tile([P, 1], F32)
-            inverse = small.tile([P, 1], F32)
-            result = results.tile([P, VOCAB], F32)
-            logits = []
+        def logits(i):
             for half in range(HALVES):
                 bank = psum_logits.tile([P, BANK], F32, tag="logits%d" % half)
-                logits.append(bank)
                 nc.tensor.matmul_mx(
                     out=bank[:],
-                    lhsT=h_codes[:].bitcast(FP8X4),
-                    lhsT_scale=h_scales[:],
+                    lhsT=live["h_codes", i][:].bitcast(FP8X4),
+                    lhsT_scale=live["h_scales", i][:],
                     rhs=w2_codes[:, BANK * half : BANK * (half + 1)].bitcast(FP8X4),
                     rhs_scale=w2_planes[4 * half : P, :],
                     start=True,
                     stop=True,
                 )
-                nc.vector.tensor_reduce(out=maxima[:, half : half + 1], in_=bank[:], axis=AXIS.X, op=ALU.max)
+                live["logits", i, half] = bank
+
+        def max_first_bank(i):
+            maxima = small.tile([P, HALVES], F32)
+            nc.vector.tensor_reduce(out=maxima[:, 0:1], in_=live["logits", i, 0][:], axis=AXIS.X, op=ALU.max)
+            live["maxima", i] = maxima
+
+        def max_second_bank(i):
+            maxima = live["maxima", i]
+            neg_max = small.tile([P, 1], F32)
+            nc.vector.tensor_reduce(out=maxima[:, 1:2], in_=live["logits", i, 1][:], axis=AXIS.X, op=ALU.max)
             nc.vector.tensor_scalar(
                 out=neg_max[:],
                 in0=maxima[:, 0:1],
@@ -188,22 +209,57 @@ def tile_adaptiveinputsoftmax_pb_kernel(
                 op0=ALU.max,
                 op1=ALU.mult,
             )
+            live["neg_max", i] = neg_max
+
+        def exponentials(i):
+            sums = small.tile([P, HALVES], F32)
+            result = results.tile([P, VOCAB], F32)
             for half in range(HALVES):
                 nc.scalar.activation(
                     out=result[:, BANK * half : BANK * (half + 1)],
-                    in_=logits[half][:],
+                    in_=live["logits", i, half][:],
                     func=ACT.Exp,
-                    bias=neg_max[:, 0:1],
+                    bias=live["neg_max", i][:, 0:1],
                     accum_out=sums[:, half : half + 1],
                 )
+            live["sums", i] = sums
+            live["result", i] = result
+
+        def invert_sum(i):
+            total = small.tile([P, 1], F32)
+            inverse = small.tile([P, 1], F32)
+            sums = live["sums", i]
             nc.vector.tensor_tensor(out=total[:], in0=sums[:, 0:1], in1=sums[:, 1:2], op=ALU.add)
             nc.vector.reciprocal(inverse[:], total[:])
-            nc.vector.tensor_scalar(
+            live["inverse", i] = inverse
+
+        def scale_and_store(i):
+            result = live["result", i]
+            scaler = nc.vector if i == TILES - 1 else nc.gpsimd
+            scaler.tensor_scalar(
                 out=result[:],
                 in0=result[:],
-                scalar1=inverse[:, 0:1],
+                scalar1=live["inverse", i][:, 0:1],
                 scalar2=prob[:, i : i + 1],
                 op0=ALU.mult,
                 op1=ALU.mult,
             )
             nc.sync.dma_start(out=out_rows[:, i, :], in_=result[:])
+
+        for step in range(-4, TILES + 1):
+            for stage_fn, i in (
+                (project, step + 2),
+                (copy_h, step + 2),
+                (max_first_bank, step),
+                (quantize_h, step + 1),
+                (logits, step + 1),
+                (transpose_x, step + 4),
+                (max_second_bank, step),
+                (exponentials, step),
+                (copy_x, step + 4),
+                (quantize_x, step + 3),
+                (invert_sum, step - 1),
+                (scale_and_store, step - 1),
+            ):
+                if 0 <= i < TILES:
+                    stage_fn(i)

@@ -81,7 +81,11 @@ def tile_adaptiveinputsoftmax_pb_kernel(
         w1_scale_rows = tail_proj_1_scales.bitcast(I32)
         w2_scale_rows = tail_w_1_scales.bitcast(I32)
 
-        nc.sync.dma_start(out=x_sb[:, 0, :], in_=x_rows[:, 0, :])
+        def load_x(i):
+            nc.sync.dma_start(out=x_sb[:, i, :], in_=x_rows[:, i, :])
+
+        for i in range(0, 3):
+            load_x(i)
         for quadrant in range(4):
             nc.sync.dma_start(
                 out=w1_planes_raw[32 * quadrant : 32 * quadrant + 8, :].bitcast(I32),
@@ -92,8 +96,8 @@ def tile_adaptiveinputsoftmax_pb_kernel(
                 out=w1_raw[:, g, :].bitcast(I32),
                 in_=tail_proj_1_words[g].rearrange("p n t -> p (n t)").bitcast(I32),
             )
-        for i in range(1, 4):
-            nc.sync.dma_start(out=x_sb[:, i, :], in_=x_rows[:, i, :])
+        for i in range(3, 6):
+            load_x(i)
         for quadrant in range(4):
             nc.sync.dma_start(
                 out=w2_planes[32 * quadrant : 32 * quadrant + 8, :].bitcast(I32),
@@ -104,13 +108,15 @@ def tile_adaptiveinputsoftmax_pb_kernel(
             in_=tail_w_1_words[0].rearrange("p n t -> p (n t)").bitcast(I32),
         )
         nc.sync.dma_start(out=prob_bf16[:], in_=prob_rows)
-        for i in range(4, TILES):
-            nc.sync.dma_start(out=x_sb[:, i, :], in_=x_rows[:, i, :])
+        for i in range(6, TILES):
+            load_x(i)
         nc.gpsimd.tensor_copy(out=prob[:], in_=prob_bf16[:])
+        minus_one = keep.tile([P, 1], F32)
+        nc.gpsimd.memset(minus_one[:], -1.0)
 
         nc.vector.tensor_copy(
-            out=w1_planes[:].rearrange("p (t m) -> p m t", t=PACK),
-            in_=w1_planes_raw[:].rearrange("p (m t) -> p m t", t=PACK),
+            out=w1_planes[:].rearrange("p (t m) -> p t m", t=PACK),
+            in_=w1_planes_raw[:].rearrange("p (m t) -> p t m", t=PACK),
         )
         for g in range(X_PASSES):
             nc.vector.tensor_copy(
@@ -229,37 +235,44 @@ def tile_adaptiveinputsoftmax_pb_kernel(
             total = small.tile([P, 1], F32)
             inverse = small.tile([P, 1], F32)
             sums = live["sums", i]
-            nc.vector.tensor_tensor(out=total[:], in0=sums[:, 0:1], in1=sums[:, 1:2], op=ALU.add)
-            nc.vector.reciprocal(inverse[:], total[:])
+            if i == TILES - 1:
+                nc.vector.tensor_tensor(out=total[:], in0=sums[:, 0:1], in1=sums[:, 1:2], op=ALU.add)
+                nc.vector.reciprocal(inverse[:], total[:])
+            else:
+                nc.gpsimd.tensor_tensor(out=total[:], in0=sums[:, 0:1], in1=sums[:, 1:2], op=ALU.add)
+                nc.gpsimd.tensor_tensor(out=inverse[:], in0=total[:], in1=minus_one[:], op=ALU.pow)
             live["inverse", i] = inverse
 
         def scale_and_store(i):
             result = live["result", i]
-            scaler = nc.vector if i == TILES - 1 else nc.gpsimd
-            scaler.tensor_scalar(
-                out=result[:],
-                in0=result[:],
-                scalar1=live["inverse", i][:, 0:1],
-                scalar2=prob[:, i : i + 1],
-                op0=ALU.mult,
-                op1=ALU.mult,
-            )
-            nc.sync.dma_start(out=out_rows[:, i, :], in_=result[:])
+            pieces = HALVES if i == TILES - 1 else 1
+            width = VOCAB // pieces
+            for piece in range(pieces):
+                columns = slice(width * piece, width * (piece + 1))
+                nc.vector.tensor_scalar(
+                    out=result[:, columns],
+                    in0=result[:, columns],
+                    scalar1=live["inverse", i][:, 0:1],
+                    scalar2=prob[:, i : i + 1],
+                    op0=ALU.mult,
+                    op1=ALU.mult,
+                )
+                nc.sync.dma_start(out=out_rows[:, i, columns], in_=result[:, columns])
 
-        for step in range(-4, TILES + 1):
+        for step in range(-7, TILES + 2):
             for stage_fn, i in (
-                (project, step + 2),
-                (copy_h, step + 2),
                 (max_first_bank, step),
                 (quantize_h, step + 1),
                 (logits, step + 1),
-                (transpose_x, step + 4),
                 (max_second_bank, step),
                 (exponentials, step),
-                (copy_x, step + 4),
-                (quantize_x, step + 3),
+                (project, step + 3),
+                (copy_h, step + 3),
+                (transpose_x, step + 7),
+                (copy_x, step + 7),
+                (scale_and_store, step - 2),
+                (quantize_x, step + 5),
                 (invert_sum, step - 1),
-                (scale_and_store, step - 1),
             ):
                 if 0 <= i < TILES:
                     stage_fn(i)

@@ -63,6 +63,18 @@ def tile_adaptiveinputsoftmax_pb_kernel(
         nc.vector.memset(warm_in[:], 0.0)
         nc.scalar.activation(out=warm_out[:], in_=warm_in[:], func=ACT.Exp)
 
+        warm_operand = keep.tile([P, BANK], BF16)
+        nc.vector.memset(warm_operand[:], 0.0)
+        warm_bank = psum_h.tile([P, BANK], F32, tag="h_t")
+
+        def warm_up(passes):
+            for repeat in range(passes):
+                nc.tensor.matmul(
+                    out=warm_bank[:], lhsT=warm_operand[:, 0:P], rhs=warm_operand[:], start=True, stop=True
+                )
+
+        warm_up(4)
+
         w1_planes_raw = keep.tile([P, D_TAIL], U8, align_bytes=64)
         w1_planes = keep.tile([P, D_TAIL], U8, align_bytes=64)
         w2_planes = keep.tile([P, BANK], U8, align_bytes=64)
@@ -137,6 +149,8 @@ def tile_adaptiveinputsoftmax_pb_kernel(
                         ident_f32[:],
                     )
             live["x_t", i] = x_t
+            if i < 4:
+                warm_up(1)
 
         def copy_x(i):
             x_grouped = stage.tile([P, X_PASSES, P, PACK], BF16, align_bytes=64)

@@ -152,6 +152,11 @@ def tile_adaptiveinputsoftmax_pb_kernel(
             if i < 4:
                 warm_up(1)
 
+        def transpose_pair(i):
+            if i % 2 == 0:
+                transpose_x(i)
+                transpose_x(i + 1)
+
         def copy_x(i):
             x_grouped = stage.tile([P, X_PASSES, P, PACK], BF16, align_bytes=64)
             nc.scalar.copy(
@@ -282,7 +287,7 @@ def tile_adaptiveinputsoftmax_pb_kernel(
                 (exponentials, step),
                 (project, step + 3),
                 (copy_h, step + 3),
-                (transpose_x, step + 7),
+                (transpose_pair, step + 7),
                 (copy_x, step + 7),
                 (scale_and_store, step - 2),
                 (quantize_x, step + 5),

@@ -64,7 +64,7 @@ def tile_adaptiveinputsoftmax_pb_kernel(
         nc.scalar.activation(out=warm_out[:], in_=warm_in[:], func=ACT.Exp)
 
         warm_operand = keep.tile([P, BANK], BF16)
-        nc.vector.memset(warm_operand[:], 0.0)
+        nc.vector.memset(warm_operand[:].bitcast(F32), 0.0)
         warm_bank = psum_h.tile([P, BANK], F32, tag="h_t")
 
         def warm_up(passes):
@@ -254,7 +254,7 @@ def tile_adaptiveinputsoftmax_pb_kernel(
             total = small.tile([P, 1], F32)
             inverse = small.tile([P, 1], F32)
             sums = live["sums", i]
-            if i == TILES - 1:
+            if i >= TILES - 2:
                 nc.vector.tensor_tensor(out=total[:], in0=sums[:, 0:1], in1=sums[:, 1:2], op=ALU.add)
                 nc.vector.reciprocal(inverse[:], total[:])
             else:

@@ -115,10 +115,11 @@ def tile_adaptiveinputsoftmax_pb_kernel(
                 out=w2_planes[32 * quadrant : 32 * quadrant + 8, :].bitcast(I32),
                 in_=w2_scale_rows[0, 4 * quadrant : 4 * quadrant + 4, :].rearrange("r (h n) -> h r n", h=HALVES),
             )
-        nc.sync.dma_start(
-            out=w2_codes[:].bitcast(I32),
-            in_=tail_w_1_words[0].rearrange("p n t -> p (n t)").bitcast(I32),
-        )
+        for half in range(HALVES):
+            nc.sync.dma_start(
+                out=w2_codes[:, BANK * half : BANK * (half + 1)].bitcast(I32),
+                in_=tail_w_1_words[0, :, BANK * half : BANK * (half + 1), :].rearrange("p n t -> p (n t)").bitcast(I32),
+            )
         nc.sync.dma_start(out=prob_bf16[:], in_=prob_rows)
         for i in range(6, TILES):
             load_x(i)

@@ -25,6 +25,8 @@ VOCAB = 1024
 TILES = TOKENS // P
 X_PASSES = D_MODEL // K_PASS
 HALVES = VOCAB // BANK
+ON_GPSIMD = TILES - 2
+VECTOR_COLUMNS = VOCAB // 2
 
 FLOPS = 2 * TOKENS * D_MODEL * D_TAIL + 2 * TOKENS * D_TAIL * VOCAB
 
@@ -124,8 +126,6 @@ def tile_adaptiveinputsoftmax_pb_kernel(
         for i in range(6, TILES):
             load_x(i)
         nc.gpsimd.tensor_copy(out=prob[:], in_=prob_bf16[:])
-        minus_one = keep.tile([P, 1], F32)
-        nc.gpsimd.memset(minus_one[:], -1.0)
 
         nc.vector.tensor_copy(
             out=w1_planes[:].rearrange("p (t m) -> p t m", t=PACK),
@@ -225,8 +225,11 @@ def tile_adaptiveinputsoftmax_pb_kernel(
 
         def max_second_bank(i):
             maxima = live["maxima", i]
-            neg_max = small.tile([P, 1], F32)
             nc.vector.tensor_reduce(out=maxima[:, 1:2], in_=live["logits", i, 1][:], axis=AXIS.X, op=ALU.max)
+
+        def join_maxima(i):
+            maxima = live["maxima", i]
+            neg_max = small.tile([P, 1], F32)
             nc.vector.tensor_scalar(
                 out=neg_max[:],
                 in0=maxima[:, 0:1],
@@ -251,17 +254,32 @@ def tile_adaptiveinputsoftmax_pb_kernel(
             live["sums", i] = sums
             live["result", i] = result
 
-        def invert_sum(i):
+        def add_sums(i):
             total = small.tile([P, 1], F32)
-            inverse = small.tile([P, 1], F32)
             sums = live["sums", i]
-            if i >= TILES - 2:
-                nc.vector.tensor_tensor(out=total[:], in0=sums[:, 0:1], in1=sums[:, 1:2], op=ALU.add)
-                nc.vector.reciprocal(inverse[:], total[:])
-            else:
-                nc.gpsimd.tensor_tensor(out=total[:], in0=sums[:, 0:1], in1=sums[:, 1:2], op=ALU.add)
-                nc.gpsimd.tensor_tensor(out=inverse[:], in0=total[:], in1=minus_one[:], op=ALU.pow)
+            adder = nc.gpsimd if i < ON_GPSIMD else nc.vector
+            adder.tensor_tensor(out=total[:], in0=sums[:, 0:1], in1=sums[:, 1:2], op=ALU.add)
+            live["total", i] = total
+
+        def invert(i):
+            inverse = small.tile([P, 1], F32)
+            nc.vector.reciprocal(inverse[:], live["total", i][:])
             live["inverse", i] = inverse
+
+        def scale(engine, i, columns):
+            result = live["result", i]
+            engine.tensor_scalar(
+                out=result[:, columns],
+                in0=result[:, columns],
+                scalar1=live["inverse", i][:, 0:1],
+                scalar2=prob[:, i : i + 1],
+                op0=ALU.mult,
+                op1=ALU.mult,
+            )
+
+        def scale_on_gpsimd(i):
+            if i < ON_GPSIMD:
+                scale(nc.gpsimd, i, slice(VECTOR_COLUMNS, VOCAB))
 
         def scale_and_store(i):
             result = live["result", i]
@@ -269,22 +287,17 @@ def tile_adaptiveinputsoftmax_pb_kernel(
             width = VOCAB // pieces
             for piece in range(pieces):
                 columns = slice(width * piece, width * (piece + 1))
-                nc.vector.tensor_scalar(
-                    out=result[:, columns],
-                    in0=result[:, columns],
-                    scalar1=live["inverse", i][:, 0:1],
-                    scalar2=prob[:, i : i + 1],
-                    op0=ALU.mult,
-                    op1=ALU.mult,
-                )
+                scale(nc.vector, i, slice(0, VECTOR_COLUMNS) if i < ON_GPSIMD else columns)
                 nc.sync.dma_start(out=out_rows[:, i, columns], in_=result[:, columns])
 
         for step in range(-7, TILES + 2):
             for stage_fn, i in (
+                (scale_on_gpsimd, step - 2),
                 (max_first_bank, step),
+                (max_second_bank, step),
                 (quantize_h, step + 1),
                 (logits, step + 1),
-                (max_second_bank, step),
+                (join_maxima, step),
                 (exponentials, step),
                 (project, step + 3),
                 (copy_h, step + 3),
@@ -292,7 +305,8 @@ def tile_adaptiveinputsoftmax_pb_kernel(
                 (copy_x, step + 7),
                 (scale_and_store, step - 2),
                 (quantize_x, step + 5),
-                (invert_sum, step - 1),
+                (add_sums, step - 1),
+                (invert, step - 1),
             ):
                 if 0 <= i < TILES:
                     stage_fn(i)

@@ -293,9 +293,9 @@ def tile_adaptiveinputsoftmax_pb_kernel(
         for step in range(-7, TILES + 2):
             for stage_fn, i in (
                 (scale_on_gpsimd, step - 2),
+                (quantize_h, step + 1),
                 (max_first_bank, step),
                 (max_second_bank, step),
-                (quantize_h, step + 1),
                 (logits, step + 1),
                 (join_maxima, step),
                 (exponentials, step),

@@ -26,7 +26,7 @@ TILES = TOKENS // P
 X_PASSES = D_MODEL // K_PASS
 HALVES = VOCAB // BANK
 ON_GPSIMD = TILES - 2
-VECTOR_COLUMNS = VOCAB // 2
+VECTOR_COLUMNS = VOCAB // 4
 
 FLOPS = 2 * TOKENS * D_MODEL * D_TAIL + 2 * TOKENS * D_TAIL * VOCAB
 
@@ -204,6 +204,14 @@ def tile_adaptiveinputsoftmax_pb_kernel(
             live["h_codes", i] = h_codes
             live["h_scales", i] = h_scales
 
+        def quantize_h_ahead(i):
+            if i != 1:
+                quantize_h(i)
+
+        def quantize_h_behind(i):
+            if i == 1:
+                quantize_h(i)
+
         def logits(i):
             for half in range(HALVES):
                 bank = psum_logits.tile([P, BANK], F32, tag="logits%d" % half)
@@ -293,8 +301,9 @@ def tile_adaptiveinputsoftmax_pb_kernel(
         for step in range(-7, TILES + 2):
             for stage_fn, i in (
                 (scale_on_gpsimd, step - 2),
-                (quantize_h, step + 1),
+                (quantize_h_ahead, step + 1),
                 (max_first_bank, step),
+                (quantize_h_behind, step + 1),
                 (max_second_bank, step),
                 (logits, step + 1),
                 (join_maxima, step),

@@ -26,7 +26,8 @@ TILES = TOKENS // P
 X_PASSES = D_MODEL // K_PASS
 HALVES = VOCAB // BANK
 ON_GPSIMD = TILES - 2
-VECTOR_COLUMNS = VOCAB // 4
+IN_HALVES = range(TILES - 3, TILES)
+DUMMIES_BEHIND = {0: 1, 2: 2}
 
 FLOPS = 2 * TOKENS * D_MODEL * D_TAIL + 2 * TOKENS * D_TAIL * VOCAB
 
@@ -150,8 +151,7 @@ def tile_adaptiveinputsoftmax_pb_kernel(
                         ident_f32[:],
                     )
             live["x_t", i] = x_t
-            if i < 4:
-                warm_up(1)
+            warm_up(DUMMIES_BEHIND.get(i, 0))
 
         def transpose_pair(i):
             if i % 2 == 0:
@@ -285,18 +285,26 @@ def tile_adaptiveinputsoftmax_pb_kernel(
                 op1=ALU.mult,
             )
 
+        def vector_columns(i):
+            return BANK if i in IN_HALVES else VOCAB // 4
+
         def scale_on_gpsimd(i):
             if i < ON_GPSIMD:
-                scale(nc.gpsimd, i, slice(VECTOR_COLUMNS, VOCAB))
+                scale(nc.gpsimd, i, slice(vector_columns(i), VOCAB))
+
+        def store(i, columns):
+            nc.sync.dma_start(out=out_rows[:, i, columns], in_=live["result", i][:, columns])
 
         def scale_and_store(i):
-            result = live["result", i]
-            pieces = HALVES if i == TILES - 1 else 1
-            width = VOCAB // pieces
-            for piece in range(pieces):
-                columns = slice(width * piece, width * (piece + 1))
-                scale(nc.vector, i, slice(0, VECTOR_COLUMNS) if i < ON_GPSIMD else columns)
-                nc.sync.dma_start(out=out_rows[:, i, columns], in_=result[:, columns])
+            if i in IN_HALVES:
+                for half in reversed(range(HALVES)):
+                    columns = slice(BANK * half, BANK * (half + 1))
+                    if half == 0 or i >= ON_GPSIMD:
+                        scale(nc.vector, i, columns)
+                    store(i, columns)
+            else:
+                scale(nc.vector, i, slice(0, vector_columns(i)))
+                store(i, slice(0, VOCAB))
 
         for step in range(-7, TILES + 2):
             for stage_fn, i in (

@@ -134,8 +134,8 @@ def tile_adaptiveinputsoftmax_pb_kernel(
         )
         for g in range(X_PASSES):
             nc.vector.tensor_copy(
-                out=w1_codes[:, g, :, :].bitcast(I32),
-                in_=w1_raw[:, g, :].bitcast(I32).rearrange("p (m t) -> p t m", t=PACK),
+                out=w1_codes[:, g, :, :].bitcast(I32).rearrange("p t (c i) -> p c t i", i=PACK),
+                in_=w1_raw[:, g, :].bitcast(I32).rearrange("p (c i t) -> p c t i", i=PACK, t=PACK),
             )
 
         live = {}

@@ -27,6 +27,8 @@ X_PASSES = D_MODEL // K_PASS
 HALVES = VOCAB // BANK
 ON_GPSIMD = TILES - 2
 IN_HALVES = range(TILES - 3, TILES)
+EARLY = TILES - 2
+ON_VECTOR = EARLY
 DUMMIES_BEHIND = {0: 1, 2: 2}
 
 FLOPS = 2 * TOKENS * D_MODEL * D_TAIL + 2 * TOKENS * D_TAIL * VOCAB
@@ -154,17 +156,41 @@ def tile_adaptiveinputsoftmax_pb_kernel(
             warm_up(DUMMIES_BEHIND.get(i, 0))
 
         def transpose_pair(i):
-            if i % 2 == 0:
+            if i < EARLY and i % 2 == 0:
                 transpose_x(i)
                 transpose_x(i + 1)
 
-        def copy_x(i):
+        def transpose_late(i):
+            if i >= EARLY:
+                transpose_x(i)
+
+        def copy_x(copy, i):
             x_grouped = stage.tile([P, X_PASSES, P, PACK], BF16, align_bytes=64)
-            nc.scalar.copy(
+            copy(
                 out=x_grouped[:].bitcast(F32),
                 in_=live["x_t", i][:].rearrange("p g u r -> p g r u"),
             )
             live["x_grouped", i] = x_grouped
+
+        def copy_x_early(i):
+            if i < EARLY:
+                copy_x(nc.scalar.copy, i)
+
+        def copy_x_late(i):
+            if i >= EARLY and i != ON_VECTOR:
+                copy_x(nc.scalar.copy, i)
+
+        def copy_x_on_vector(i):
+            if i == ON_VECTOR:
+                copy_x(nc.vector.tensor_copy, i)
+
+        def quantize_x_early(i):
+            if i < EARLY:
+                quantize_x(i)
+
+        def quantize_x_late(i):
+            if i >= EARLY:
+                quantize_x(i)
 
         def quantize_x(i):
             nc.vector.quantize_mx(
@@ -319,9 +345,13 @@ def tile_adaptiveinputsoftmax_pb_kernel(
                 (project, step + 3),
                 (copy_h, step + 3),
                 (transpose_pair, step + 7),
-                (copy_x, step + 7),
+                (transpose_late, step + 6),
+                (copy_x_early, step + 7),
+                (copy_x_late, step + 6),
+                (copy_x_on_vector, step + 5),
                 (scale_and_store, step - 2),
-                (quantize_x, step + 5),
+                (quantize_x_early, step + 5),
+                (quantize_x_late, step + 4),
                 (add_sums, step - 1),
                 (invert, step - 1),
             ):

@@ -29,6 +29,7 @@ ON_GPSIMD = TILES - 2
 IN_HALVES = range(TILES - 3, TILES)
 EARLY = TILES - 2
 ON_VECTOR = EARLY
+GROUPED = range(4, EARLY)
 DUMMIES_BEHIND = {0: 1, 2: 2}
 
 FLOPS = 2 * TOKENS * D_MODEL * D_TAIL + 2 * TOKENS * D_TAIL * VOCAB
@@ -142,16 +143,23 @@ def tile_adaptiveinputsoftmax_pb_kernel(
 
         live = {}
 
+        def group_words(i):
+            if i in GROUPED:
+                words = stage.tile([P, X_PASSES, 2, P], I32)
+                nc.vector.tensor_copy(
+                    out=words[:], in_=x_sb[:, i, :].bitcast(I32).rearrange("p (g w u) -> p g u w", g=X_PASSES, u=2)
+                )
+                live["words", i] = words
+
         def transpose_x(i):
-            x_words = x_sb[:, i, :].bitcast(F32)
             x_t = psum_x.tile([P, X_PASSES, 2, P], F32)
             for g in range(X_PASSES):
                 for u in range(2):
-                    nc.tensor.transpose(
-                        x_t[:, g, u, :],
-                        x_words[:, 256 * g + u : 256 * (g + 1) : 2],
-                        ident_f32[:],
-                    )
+                    if i in GROUPED:
+                        words = live["words", i][:, g, u, :].bitcast(F32)
+                    else:
+                        words = x_sb[:, i, :].bitcast(F32)[:, 256 * g + u : 256 * (g + 1) : 2]
+                    nc.tensor.transpose(x_t[:, g, u, :], words, ident_f32[:])
             live["x_t", i] = x_t
             warm_up(DUMMIES_BEHIND.get(i, 0))
 
@@ -344,6 +352,7 @@ def tile_adaptiveinputsoftmax_pb_kernel(
                 (exponentials, step),
                 (project, step + 3),
                 (copy_h, step + 3),
+                (group_words, step + 8),
                 (transpose_pair, step + 7),
                 (transpose_late, step + 6),
                 (copy_x_early, step + 7),

from contextlib import ExitStack

import concourse.mybir as mybir
from concourse.masks import make_identity

F32 = mybir.dt.float32
BF16 = mybir.dt.bfloat16
I32 = mybir.dt.int32
U32 = mybir.dt.uint32
U8 = mybir.dt.uint8
FP8X4 = mybir.dt.float8_e4m3fn_x4
ALU = mybir.AluOpType
ACT = mybir.ActivationFunctionType
AXIS = mybir.AxisListType

P = 128
PACK = 4
K_PASS = P * PACK
BANK = 512

TOKENS = 1024
D_MODEL = 1024
D_TAIL = 512
VOCAB = 1024
TILES = TOKENS // P
X_PASSES = D_MODEL // K_PASS
HALVES = VOCAB // BANK
ON_GPSIMD = TILES - 2
IN_HALVES = range(TILES - 3, TILES)
EARLY = TILES - 2
ON_VECTOR = EARLY
GROUPED = range(4, EARLY)
DUMMIES_BEHIND = {0: 1, 2: 2}

FLOPS = 2 * TOKENS * D_MODEL * D_TAIL + 2 * TOKENS * D_TAIL * VOCAB


def tile_adaptiveinputsoftmax_pb_kernel(
    tc,
    x,
    tail_proj_1_words,
    tail_proj_1_scales,
    tail_w_1_words,
    tail_w_1_scales,
    cluster_prob,
    out,
):
    nc = tc.nc

    x_rows = x.flatten_outer_dims().rearrange("(p j) d -> p j d", j=TILES)
    out_rows = out.flatten_outer_dims().rearrange("(p j) v -> p j v", j=TILES)
    prob_rows = cluster_prob.flatten_outer_dims().rearrange("(p j) o -> p (j o)", j=TILES)

    with ExitStack() as ctx:
        keep = ctx.enter_context(tc.tile_pool(name="keep", bufs=1))
        stage = ctx.enter_context(tc.tile_pool(name="stage", bufs=4))
        small = ctx.enter_context(tc.tile_pool(name="small", bufs=4))
        results = ctx.enter_context(tc.tile_pool(name="results", bufs=8))
        psum_x = ctx.enter_context(tc.psum_pool(name="psum_x", bufs=2))
        psum_h = ctx.enter_context(tc.psum_pool(name="psum_h", bufs=2))
        psum_logits = ctx.enter_context(tc.psum_pool(name="psum_logits", bufs=2))
        ctx.enter_context(tc.manual_schedule())

        ident_f32 = keep.tile([P, P], F32)
        make_identity(nc, ident_f32[:])

        warm_in = keep.tile([P, 1], F32)
        warm_out = keep.tile([P, 1], F32)
        nc.vector.memset(warm_in[:], 0.0)
        nc.scalar.activation(out=warm_out[:], in_=warm_in[:], func=ACT.Exp)

        warm_operand = keep.tile([P, BANK], BF16)
        nc.vector.memset(warm_operand[:].bitcast(F32), 0.0)
        warm_bank = psum_h.tile([P, BANK], F32, tag="h_t")

        def warm_up(passes):
            for repeat in range(passes):
                nc.tensor.matmul(
                    out=warm_bank[:], lhsT=warm_operand[:, 0:P], rhs=warm_operand[:], start=True, stop=True
                )

        warm_up(4)

        w1_planes_raw = keep.tile([P, D_TAIL], U8, align_bytes=64)
        w1_planes = keep.tile([P, D_TAIL], U8, align_bytes=64)
        w2_planes = keep.tile([P, BANK], U8, align_bytes=64)
        nc.vector.memset(w1_planes_raw[:].bitcast(I32), 0)
        nc.vector.memset(w2_planes[:].bitcast(I32), 0)

        x_sb = keep.tile([P, TILES, D_MODEL], BF16)
        w1_raw = keep.tile([P, X_PASSES, D_TAIL], U32, align_bytes=64)
        w1_codes = keep.tile([P, X_PASSES, PACK, P], U32, align_bytes=64)
        w2_codes = keep.tile([P, VOCAB], U32, align_bytes=64)
        prob_bf16 = keep.tile([P, TILES], BF16)
        prob = keep.tile([P, TILES], F32)
        x_codes = keep.tile([P, TILES, X_PASSES, P], U32, align_bytes=64)
        x_scales = keep.tile([P, TILES, X_PASSES, P], U8, align_bytes=64)

        w1_scale_rows = tail_proj_1_scales.bitcast(I32)
        w2_scale_rows = tail_w_1_scales.bitcast(I32)

        def load_x(i):
            nc.sync.dma_start(out=x_sb[:, i, :], in_=x_rows[:, i, :])

        for i in range(0, 3):
            load_x(i)
        for quadrant in range(4):
            nc.sync.dma_start(
                out=w1_planes_raw[32 * quadrant : 32 * quadrant + 8, :].bitcast(I32),
                in_=w1_scale_rows[:, 4 * quadrant : 4 * quadrant + 4, :],
            )
        for g in range(X_PASSES):
            nc.sync.dma_start(
                out=w1_raw[:, g, :].bitcast(I32),
                in_=tail_proj_1_words[g].rearrange("p n t -> p (n t)").bitcast(I32),
            )
        for i in range(3, 6):
            load_x(i)
        for quadrant in range(4):
            nc.sync.dma_start(
                out=w2_planes[32 * quadrant : 32 * quadrant + 8, :].bitcast(I32),
                in_=w2_scale_rows[0, 4 * quadrant : 4 * quadrant + 4, :].rearrange("r (h n) -> h r n", h=HALVES),
            )
        for half in range(HALVES):
            nc.sync.dma_start(
                out=w2_codes[:, BANK * half : BANK * (half + 1)].bitcast(I32),
                in_=tail_w_1_words[0, :, BANK * half : BANK * (half + 1), :].rearrange("p n t -> p (n t)").bitcast(I32),
            )
        nc.sync.dma_start(out=prob_bf16[:], in_=prob_rows)
        for i in range(6, TILES):
            load_x(i)
        nc.gpsimd.tensor_copy(out=prob[:], in_=prob_bf16[:])

        nc.vector.tensor_copy(
            out=w1_planes[:].rearrange("p (t m) -> p t m", t=PACK),
            in_=w1_planes_raw[:].rearrange("p (m t) -> p t m", t=PACK),
        )
        for g in range(X_PASSES):
            nc.vector.tensor_copy(
                out=w1_codes[:, g, :, :].bitcast(I32).rearrange("p t (c i) -> p c t i", i=PACK),
                in_=w1_raw[:, g, :].bitcast(I32).rearrange("p (c i t) -> p c t i", i=PACK, t=PACK),
            )

        live = {}

        def group_words(i):
            if i in GROUPED:
                words = stage.tile([P, X_PASSES, 2, P], I32)
                nc.vector.tensor_copy(
                    out=words[:], in_=x_sb[:, i, :].bitcast(I32).rearrange("p (g w u) -> p g u w", g=X_PASSES, u=2)
                )
                live["words", i] = words

        def transpose_x(i):
            x_t = psum_x.tile([P, X_PASSES, 2, P], F32)
            for g in range(X_PASSES):
                for u in range(2):
                    if i in GROUPED:
                        words = live["words", i][:, g, u, :].bitcast(F32)
                    else:
                        words = x_sb[:, i, :].bitcast(F32)[:, 256 * g + u : 256 * (g + 1) : 2]
                    nc.tensor.transpose(x_t[:, g, u, :], words, ident_f32[:])
            live["x_t", i] = x_t
            warm_up(DUMMIES_BEHIND.get(i, 0))

        def transpose_pair(i):
            if i < EARLY and i % 2 == 0:
                transpose_x(i)
                transpose_x(i + 1)

        def transpose_late(i):
            if i >= EARLY:
                transpose_x(i)

        def copy_x(copy, i):
            x_grouped = stage.tile([P, X_PASSES, P, PACK], BF16, align_bytes=64)
            copy(
                out=x_grouped[:].bitcast(F32),
                in_=live["x_t", i][:].rearrange("p g u r -> p g r u"),
            )
            live["x_grouped", i] = x_grouped

        def copy_x_early(i):
            if i < EARLY:
                copy_x(nc.scalar.copy, i)

        def copy_x_late(i):
            if i >= EARLY and i != ON_VECTOR:
                copy_x(nc.scalar.copy, i)

        def copy_x_on_vector(i):
            if i == ON_VECTOR:
                copy_x(nc.vector.tensor_copy, i)

        def quantize_x_early(i):
            if i < EARLY:
                quantize_x(i)

        def quantize_x_late(i):
            if i >= EARLY:
                quantize_x(i)

        def quantize_x(i):
            nc.vector.quantize_mx(
                out=x_codes[:, i, :, :].rearrange("p g r -> p (g r)").bitcast(FP8X4),
                scales=x_scales[:, i, :, :].rearrange("p g r -> p (g r)"),
                in_=live["x_grouped", i][:].rearrange("p g r t -> p (g r t)"),
            )

        def project(i):
            h_t = psum_h.tile([P, PACK, P], F32)
            for t in range(PACK):
                for g in range(X_PASSES):
                    nc.tensor.matmul_mx(
                        out=h_t[:, t, :],
                        lhsT=w1_codes[:, g, t, :].bitcast(FP8X4),
                        lhsT_scale=w1_planes[4 * g : P, P * t : P * (t + 1)],
                        rhs=x_codes[:, i, g, :].bitcast(FP8X4),
                        rhs_scale=x_scales[:, i, g, :],
                        start=(g == 0),
                        stop=(g == X_PASSES - 1),
                    )
            live["h_t", i] = h_t

        def copy_h(i):
            h_grouped = stage.tile([P, P, PACK], BF16, align_bytes=64)
            nc.scalar.copy(out=h_grouped[:], in_=live["h_t", i][:].rearrange("p t r -> p r t"))
            live["h_grouped", i] = h_grouped

        def quantize_h(i):
            h_codes = stage.tile([P, P], U32, align_bytes=64)
            h_scales = stage.tile([P, P], U8, align_bytes=64)
            nc.vector.quantize_mx(
                out=h_codes[:].bitcast(FP8X4),
                scales=h_scales[:],
                in_=live["h_grouped", i][:].rearrange("p r t -> p (r t)"),
            )
            live["h_codes", i] = h_codes
            live["h_scales", i] = h_scales

        def quantize_h_ahead(i):
            if i != 1:
                quantize_h(i)

        def quantize_h_behind(i):
            if i == 1:
                quantize_h(i)

        def logits(i):
            for half in range(HALVES):
                bank = psum_logits.tile([P, BANK], F32, tag="logits%d" % half)
                nc.tensor.matmul_mx(
                    out=bank[:],
                    lhsT=live["h_codes", i][:].bitcast(FP8X4),
                    lhsT_scale=live["h_scales", i][:],
                    rhs=w2_codes[:, BANK * half : BANK * (half + 1)].bitcast(FP8X4),
                    rhs_scale=w2_planes[4 * half : P, :],
                    start=True,
                    stop=True,
                )
                live["logits", i, half] = bank

        def max_first_bank(i):
            maxima = small.tile([P, HALVES], F32)
            nc.vector.tensor_reduce(out=maxima[:, 0:1], in_=live["logits", i, 0][:], axis=AXIS.X, op=ALU.max)
            live["maxima", i] = maxima

        def max_second_bank(i):
            maxima = live["maxima", i]
            nc.vector.tensor_reduce(out=maxima[:, 1:2], in_=live["logits", i, 1][:], axis=AXIS.X, op=ALU.max)

        def join_maxima(i):
            maxima = live["maxima", i]
            neg_max = small.tile([P, 1], F32)
            nc.vector.tensor_scalar(
                out=neg_max[:],
                in0=maxima[:, 0:1],
                scalar1=maxima[:, 1:2],
                scalar2=-1.0,
                op0=ALU.max,
                op1=ALU.mult,
            )
            live["neg_max", i] = neg_max

        def exponentials(i):
            sums = small.tile([P, HALVES], F32)
            result = results.tile([P, VOCAB], F32)
            for half in range(HALVES):
                nc.scalar.activation(
                    out=result[:, BANK * half : BANK * (half + 1)],
                    in_=live["logits", i, half][:],
                    func=ACT.Exp,
                    bias=live["neg_max", i][:, 0:1],
                    accum_out=sums[:, half : half + 1],
                )
            live["sums", i] = sums
            live["result", i] = result

        def add_sums(i):
            total = small.tile([P, 1], F32)
            sums = live["sums", i]
            adder = nc.gpsimd if i < ON_GPSIMD else nc.vector
            adder.tensor_tensor(out=total[:], in0=sums[:, 0:1], in1=sums[:, 1:2], op=ALU.add)
            live["total", i] = total

        def invert(i):
            inverse = small.tile([P, 1], F32)
            nc.vector.reciprocal(inverse[:], live["total", i][:])
            live["inverse", i] = inverse

        def scale(engine, i, columns):
            result = live["result", i]
            engine.tensor_scalar(
                out=result[:, columns],
                in0=result[:, columns],
                scalar1=live["inverse", i][:, 0:1],
                scalar2=prob[:, i : i + 1],
                op0=ALU.mult,
                op1=ALU.mult,
            )

        def vector_columns(i):
            return BANK if i in IN_HALVES else VOCAB // 4

        def scale_on_gpsimd(i):
            if i < ON_GPSIMD:
                scale(nc.gpsimd, i, slice(vector_columns(i), VOCAB))

        def store(i, columns):
            nc.sync.dma_start(out=out_rows[:, i, columns], in_=live["result", i][:, columns])

        def scale_and_store(i):
            if i in IN_HALVES:
                for half in reversed(range(HALVES)):
                    columns = slice(BANK * half, BANK * (half + 1))
                    if half == 0 or i >= ON_GPSIMD:
                        scale(nc.vector, i, columns)
                    store(i, columns)
            else:
                scale(nc.vector, i, slice(0, vector_columns(i)))
                store(i, slice(0, VOCAB))

        for step in range(-7, TILES + 2):
            for stage_fn, i in (
                (scale_on_gpsimd, step - 2),
                (quantize_h_ahead, step + 1),
                (max_first_bank, step),
                (quantize_h_behind, step + 1),
                (max_second_bank, step),
                (logits, step + 1),
                (join_maxima, step),
                (exponentials, step),
                (project, step + 3),
                (copy_h, step + 3),
                (group_words, step + 8),
                (transpose_pair, step + 7),
                (transpose_late, step + 6),
                (copy_x_early, step + 7),
                (copy_x_late, step + 6),
                (copy_x_on_vector, step + 5),
                (scale_and_store, step - 2),
                (quantize_x_early, step + 5),
                (quantize_x_late, step + 4),
                (add_sums, step - 1),
                (invert, step - 1),
            ):
                if 0 <= i < TILES:
                    stage_fn(i)
